import numpy as np
import ml_dtypes


def mxq(x, axis, fmt="e4m3"):
    dtype, down = {"e4m3": (ml_dtypes.float8_e4m3fn, 7), "e5m2": (ml_dtypes.float8_e5m2, 14)}[fmt]
    v = np.moveaxis(np.asarray(x, np.float32).astype(ml_dtypes.bfloat16).astype(np.float64), axis, -1)
    blocks = v.reshape(v.shape[:-1] + (-1, 32))
    amax = np.abs(blocks).max(-1, keepdims=True)
    byte = np.maximum(np.where(amax > 0, np.frexp(amax)[1] - 1 + 127, 0) - down, 1)
    scale = np.exp2(byte - 127.0)
    codes = (blocks / scale).astype(np.float32).astype(dtype).astype(np.float64)
    return np.moveaxis((codes * scale).reshape(v.shape), -1, axis)


BF16 = ml_dtypes.bfloat16


def bf(x):
    return np.asarray(x, np.float32).astype(BF16)


def f64(x):
    return np.asarray(x).astype(np.float64)


B, N, SHOT, D = 512, 256, 5, 1024
C = 2.0


def setup_inputs():
    g = np.random.standard_normal(D) * C
    x1 = (g + np.random.standard_normal((B, D))) / np.sqrt(D)
    x2 = (g + np.random.standard_normal((N, SHOT, D)) * np.sqrt(SHOT)) / np.sqrt(D)
    return {"x1": bf(x1.reshape(B, D, 1, 1)), "x2": bf(x2.reshape(N, SHOT, D, 1, 1))}


def reference(x1, x2):
    x1, x2 = f64(x1), f64(x2)
    b = x1.shape[0]
    q = x1.reshape(b, -1)
    n = x2.shape[0]
    protos = x2.reshape(n, x2.shape[1], -1).mean(axis=1)
    q_sq = np.sum(q * q, axis=-1, keepdims=True)
    p_sq = np.sum(protos * protos, axis=-1)
    cross = mxq(q, 1, "e4m3") @ mxq(protos, 1, "e4m3").T
    score = -(q_sq - 2.0 * cross + p_sq[None, :])
    return score

@@ -1,0 +1,167 @@
+import concourse.mybir as mybir
+from concourse.masks import make_identity
+
+F32 = mybir.dt.float32
+BF16 = mybir.dt.bfloat16
+U32 = mybir.dt.uint32
+U8 = mybir.dt.uint8
+FP8X4 = mybir.dt.float8_e4m3fn_x4
+ALU = mybir.AluOpType
+ACT = mybir.ActivationFunctionType
+
+P = 128
+PACK = 4
+K_PASS = P * PACK
+
+B, N, SHOT, D = 512, 256, 5, 1024
+Q_TILES = B // P
+N_TILES = N // P
+PASSES = D // K_PASS
+HALVES = 2
+PAIR = 2
+
+FLOPS = 2 * B * N * D
+
+
+def tile_proto_metric_s_kernel(tc, x1, x2, out):
+    nc = tc.nc
+
+    x1_rows = x1.rearrange("(p t) d a b -> p (t d a b)", t=Q_TILES)
+    x2_rows = x2.rearrange("(t p) s d a b -> t p s (d a b)", p=P)
+    out_rows = out.rearrange("(p t) j -> p t j", t=Q_TILES)
+
+    with tc.tile_pool(name="keep", bufs=1) as keep, tc.psum_pool(name="psum", bufs=2) as psum:
+        x1_sb = keep.tile([P, Q_TILES * D], BF16)
+        x2_sb = keep.tile([P, N_TILES, SHOT, D], BF16)
+
+        half_x1 = Q_TILES * D // 2
+        nc.sync.dma_start(out=x2_sb[:, 0, 0:2, :], in_=x2_rows[0][:, 0:2, :])
+        nc.sync.dma_start(out=x1_sb[:, 0:half_x1], in_=x1_rows[:, 0:half_x1])
+        nc.sync.dma_start(out=x2_sb[:, 0, 2:SHOT, :], in_=x2_rows[0][:, 2:SHOT, :])
+        nc.sync.dma_start(out=x1_sb[:, half_x1:], in_=x1_rows[:, half_x1:])
+        nc.sync.dma_start(out=x2_sb[:, 1, 0:2, :], in_=x2_rows[1][:, 0:2, :])
+        nc.sync.dma_start(out=x2_sb[:, 1, 2:SHOT, :], in_=x2_rows[1][:, 2:SHOT, :])
+
+        ident = keep.tile([P, P], F32)
+        make_identity(nc, ident[:])
+
+        total = keep.tile([P, N_TILES, D], F32)
+        other = keep.tile([P, N_TILES, D], F32)
+        q_squares = keep.tile([P, Q_TILES * D], BF16)
+        p_squares = keep.tile([P, N_TILES, D], BF16)
+        q_sq = keep.tile([P, Q_TILES], F32)
+        p_sq_parts = keep.tile([P, N_TILES, PASSES], F32)
+        q_grouped = keep.tile([P, Q_TILES * PASSES * P * PACK], BF16, align_bytes=64)
+        q_codes = keep.tile([P, Q_TILES, PASSES, P], U32, align_bytes=64)
+        q_scales = keep.tile([P, Q_TILES, PASSES, P], U8, align_bytes=64)
+        p_grouped = keep.tile([P, N_TILES, PASSES, P, PACK], BF16, align_bytes=64)
+        p_codes = keep.tile([P, N_TILES, PASSES, P], U32, align_bytes=64)
+        p_scales = keep.tile([P, N_TILES, PASSES, P], U8, align_bytes=64)
+
+        x1_words = x1_sb[:].bitcast(F32).rearrange(
+            "p (t c u w) -> p t c u w", t=Q_TILES, c=PASSES, u=HALVES
+        )
+        q_grouped_words = q_grouped[:].bitcast(F32).rearrange(
+            "p (t c i u) -> p t c i u", t=Q_TILES, c=PASSES, u=HALVES
+        )
+        q_grouped_tiles = q_grouped[:].rearrange("p (t k) -> p t k", t=Q_TILES)
+        x1_tiles = x1_sb[:].rearrange("p (t d) -> p t d", t=Q_TILES)
+        q_squares_tiles = q_squares[:].rearrange("p (t d) -> p t d", t=Q_TILES)
+        total_features = total[:].rearrange(
+            "p t (c u w e) -> p t c u w e", c=PASSES, u=HALVES, e=PAIR
+        )
+
+        def pass_cols(c):
+            return slice(c * K_PASS, (c + 1) * K_PASS)
+
+        def add_shots(t, dst, in0, in1):
+            for c in range(PASSES):
+                nc.vector.tensor_tensor(
+                    out=dst[:, t, pass_cols(c)], in0=in0[:, pass_cols(c)], in1=in1[:, pass_cols(c)],
+                    op=ALU.add,
+                )
+
+        def sum_shots(t):
+            shots = x2_sb[:, t]
+            add_shots(t, total, shots[:, 0, :], shots[:, 1, :])
+            add_shots(t, other, shots[:, 2, :], shots[:, 3, :])
+            add_shots(t, total, total[:, t, :], other[:, t, :])
+            add_shots(t, total, total[:, t, :], shots[:, 4, :])
+
+        def prepare_queries(t):
+            nc.scalar.activation(
+                out=q_squares_tiles[:, t, :], in_=x1_tiles[:, t, :], func=ACT.Square,
+                accum_out=q_sq[:, t : t + 1],
+            )
+            q_t = psum.tile([P, PASSES, HALVES, P], F32)
+            for c in range(PASSES):
+                for u in range(HALVES):
+                    nc.tensor.transpose(out=q_t[:, c, u, :], in_=x1_words[:, t, c, u, :], identity=ident[:])
+            nc.scalar.copy(out=q_grouped_words[:, t], in_=q_t[:].rearrange("p c u i -> p c i u"))
+            nc.vector.quantize_mx(
+                out=q_codes[:, t].rearrange("p c i -> p (c i)").bitcast(FP8X4),
+                scales=q_scales[:, t].rearrange("p c i -> p (c i)"),
+                in_=q_grouped_tiles[:, t, :],
+            )
+
+        def prepare_protos(t, c):
+            nc.scalar.activation(
+                out=p_squares[:, t, pass_cols(c)], in_=total[:, t, pass_cols(c)], func=ACT.Square,
+                scale=1.0 / SHOT, accum_out=p_sq_parts[:, t, c : c + 1],
+            )
+            p_t = psum.tile([P, HALVES, PAIR, P], F32)
+            for u in range(HALVES):
+                for e in range(PAIR):
+                    nc.tensor.transpose(
+                        out=p_t[:, u, e, :], in_=total_features[:, t, c, u, :, e], identity=ident[:]
+                    )
+            nc.scalar.activation(
+                out=p_grouped[:, t, c], in_=p_t[:].rearrange("p u e j -> p j (u e)"), func=ACT.Copy,
+                scale=1.0 / SHOT,
+            )
+            nc.vector.quantize_mx(
+                out=p_codes[:, t, c, :].bitcast(FP8X4),
+                scales=p_scales[:, t, c, :],
+                in_=p_grouped[:, t, c].rearrange("p j f -> p (j f)"),
+            )
+
+        def scores(t):
+            repeated = keep.tile([P, P], F32, name="repeated%d" % t)
+            nc.scalar.activation(
+                out=repeated[:], in_=p_sq_parts[:, t, 0:1].to_broadcast([P, P]), func=ACT.Identity,
+                bias=p_sq_parts[:, t, 1:2], scale=1.0,
+            )
+            p_sq_rows = psum.tile([P, P], F32)
+            nc.tensor.transpose(out=p_sq_rows[:], in_=repeated[:], identity=ident[:])
+            norms = keep.tile([P, Q_TILES, P], F32, name="norms%d" % t)
+            nc.vector.tensor_tensor(
+                out=norms[:],
+                in0=p_sq_rows[:].unsqueeze(1).to_broadcast([P, Q_TILES, P]),
+                in1=q_sq[:].unsqueeze(2).to_broadcast([P, Q_TILES, P]),
+                op=ALU.add,
+            )
+            cross = psum.tile([P, Q_TILES, P], F32)
+            for i in range(Q_TILES):
+                for c in range(PASSES):
+                    nc.tensor.matmul_mx(
+                        out=cross[:, i, :],
+                        lhsT=q_codes[:, i, c, :].bitcast(FP8X4),
+                        lhsT_scale=q_scales[:, i, c, :],
+                        rhs=p_codes[:, t, c, :].bitcast(FP8X4),
+                        rhs_scale=p_scales[:, t, c, :],
+                        start=(c == 0),
+                        stop=(c == PASSES - 1),
+                    )
+            score = keep.tile([P, Q_TILES, P], F32, name="score%d" % t)
+            nc.vector.scalar_tensor_tensor(
+                out=score[:], in0=cross[:], scalar=2.0, in1=norms[:], op0=ALU.mult, op1=ALU.subtract
+            )
+            nc.sync.dma_start(out=out_rows[:, :, t * P : (t + 1) * P], in_=score[:])
+
+        for t in range(Q_TILES):
+            prepare_queries(t)
+        for t in range(N_TILES):
+            sum_shots(t)
+            for c in range(PASSES):
+                prepare_protos(t, c)
+            scores(t)

@@ -34,23 +34,21 @@ def tile_proto_metric_s_kernel(tc, x1, x2, out):
         x1_sb = keep.tile([P, Q_TILES * D], BF16)
         x2_sb = keep.tile([P, N_TILES, SHOT, D], BF16)
 
-        half_x1 = Q_TILES * D // 2
-        nc.sync.dma_start(out=x2_sb[:, 0, 0:2, :], in_=x2_rows[0][:, 0:2, :])
-        nc.sync.dma_start(out=x1_sb[:, 0:half_x1], in_=x1_rows[:, 0:half_x1])
-        nc.sync.dma_start(out=x2_sb[:, 0, 2:SHOT, :], in_=x2_rows[0][:, 2:SHOT, :])
-        nc.sync.dma_start(out=x1_sb[:, half_x1:], in_=x1_rows[:, half_x1:])
-        nc.sync.dma_start(out=x2_sb[:, 1, 0:2, :], in_=x2_rows[1][:, 0:2, :])
-        nc.sync.dma_start(out=x2_sb[:, 1, 2:SHOT, :], in_=x2_rows[1][:, 2:SHOT, :])
+        for t in range(N_TILES):
+            for s in range(SHOT):
+                nc.sync.dma_start(out=x2_sb[:, t, s, :], in_=x2_rows[t][:, s, :])
+                if t == 0 and s > 0:
+                    k = s - 1
+                    nc.sync.dma_start(out=x1_sb[:, k * D : (k + 1) * D], in_=x1_rows[:, k * D : (k + 1) * D])
 
         ident = keep.tile([P, P], F32)
         make_identity(nc, ident[:])
 
         total = keep.tile([P, N_TILES, D], F32)
-        other = keep.tile([P, N_TILES, D], F32)
         q_squares = keep.tile([P, Q_TILES * D], BF16)
         p_squares = keep.tile([P, N_TILES, D], BF16)
         q_sq = keep.tile([P, Q_TILES], F32)
-        p_sq_parts = keep.tile([P, N_TILES, PASSES], F32)
+        p_sq = keep.tile([P, N_TILES], F32)
         q_grouped = keep.tile([P, Q_TILES * PASSES * P * PACK], BF16, align_bytes=64)
         q_codes = keep.tile([P, Q_TILES, PASSES, P], U32, align_bytes=64)
         q_scales = keep.tile([P, Q_TILES, PASSES, P], U8, align_bytes=64)
@@ -74,19 +72,13 @@ def tile_proto_metric_s_kernel(tc, x1, x2, out):
         def pass_cols(c):
             return slice(c * K_PASS, (c + 1) * K_PASS)
 
-        def add_shots(t, dst, in0, in1):
-            for c in range(PASSES):
-                nc.vector.tensor_tensor(
-                    out=dst[:, t, pass_cols(c)], in0=in0[:, pass_cols(c)], in1=in1[:, pass_cols(c)],
-                    op=ALU.add,
-                )
-
         def sum_shots(t):
-            shots = x2_sb[:, t]
-            add_shots(t, total, shots[:, 0, :], shots[:, 1, :])
-            add_shots(t, other, shots[:, 2, :], shots[:, 3, :])
-            add_shots(t, total, total[:, t, :], other[:, t, :])
-            add_shots(t, total, total[:, t, :], shots[:, 4, :])
+            for s in range(1, SHOT):
+                for c in range(PASSES):
+                    so_far = x2_sb[:, t, 0, pass_cols(c)] if s == 1 else total[:, t, pass_cols(c)]
+                    nc.vector.tensor_tensor(
+                        out=total[:, t, pass_cols(c)], in0=so_far, in1=x2_sb[:, t, s, pass_cols(c)], op=ALU.add
+                    )
 
         def prepare_queries(t):
             nc.scalar.activation(
@@ -105,10 +97,6 @@ def tile_proto_metric_s_kernel(tc, x1, x2, out):
             )
 
         def prepare_protos(t, c):
-            nc.scalar.activation(
-                out=p_squares[:, t, pass_cols(c)], in_=total[:, t, pass_cols(c)], func=ACT.Square,
-                scale=1.0 / SHOT, accum_out=p_sq_parts[:, t, c : c + 1],
-            )
             p_t = psum.tile([P, HALVES, PAIR, P], F32)
             for u in range(HALVES):
                 for e in range(PAIR):
@@ -126,13 +114,14 @@ def tile_proto_metric_s_kernel(tc, x1, x2, out):
             )
 
         def scores(t):
-            repeated = keep.tile([P, P], F32, name="repeated%d" % t)
             nc.scalar.activation(
-                out=repeated[:], in_=p_sq_parts[:, t, 0:1].to_broadcast([P, P]), func=ACT.Identity,
-                bias=p_sq_parts[:, t, 1:2], scale=1.0,
+                out=p_squares[:, t, :], in_=total[:, t, :], func=ACT.Square,
+                scale=1.0 / SHOT, accum_out=p_sq[:, t : t + 1],
             )
             p_sq_rows = psum.tile([P, P], F32)
-            nc.tensor.transpose(out=p_sq_rows[:], in_=repeated[:], identity=ident[:])
+            nc.tensor.transpose(
+                out=p_sq_rows[:], in_=p_sq[:, t : t + 1].to_broadcast([P, P]), identity=ident[:]
+            )
             norms = keep.tile([P, Q_TILES, P], F32, name="norms%d" % t)
             nc.vector.tensor_tensor(
                 out=norms[:],
@@ -158,10 +147,11 @@ def tile_proto_metric_s_kernel(tc, x1, x2, out):
             )
             nc.sync.dma_start(out=out_rows[:, :, t * P : (t + 1) * P], in_=score[:])
 
-        for t in range(Q_TILES):
-            prepare_queries(t)
         for t in range(N_TILES):
             sum_shots(t)
             for c in range(PASSES):
                 prepare_protos(t, c)
+        for t in range(Q_TILES):
+            prepare_queries(t)
+        for t in range(N_TILES):
             scores(t)

@@ -20,6 +20,8 @@ PASSES = D // K_PASS
 HALVES = 2
 PAIR = 2
 
+QUANT_LAG = 2
+
 FLOPS = 2 * B * N * D
 
 
@@ -33,22 +35,15 @@ def tile_proto_metric_s_kernel(tc, x1, x2, out):
     with tc.tile_pool(name="keep", bufs=1) as keep, tc.psum_pool(name="psum", bufs=2) as psum:
         x1_sb = keep.tile([P, Q_TILES * D], BF16)
         x2_sb = keep.tile([P, N_TILES, SHOT, D], BF16)
-
-        for t in range(N_TILES):
-            for s in range(SHOT):
-                nc.sync.dma_start(out=x2_sb[:, t, s, :], in_=x2_rows[t][:, s, :])
-                if t == 0 and s > 0:
-                    k = s - 1
-                    nc.sync.dma_start(out=x1_sb[:, k * D : (k + 1) * D], in_=x1_rows[:, k * D : (k + 1) * D])
-
         ident = keep.tile([P, P], F32)
-        make_identity(nc, ident[:])
-
         total = keep.tile([P, N_TILES, D], F32)
         q_squares = keep.tile([P, Q_TILES * D], BF16)
         p_squares = keep.tile([P, N_TILES, D], BF16)
         q_sq = keep.tile([P, Q_TILES], F32)
-        p_sq = keep.tile([P, N_TILES], F32)
+        p_sq_parts = keep.tile([P, N_TILES, PASSES], F32)
+        p_sq_repeated = keep.tile([P, N_TILES, P], F32)
+        norms = keep.tile([P, N_TILES, Q_TILES, P], F32)
+        score = keep.tile([P, N_TILES, Q_TILES, P], F32)
         q_grouped = keep.tile([P, Q_TILES * PASSES * P * PACK], BF16, align_bytes=64)
         q_codes = keep.tile([P, Q_TILES, PASSES, P], U32, align_bytes=64)
         q_scales = keep.tile([P, Q_TILES, PASSES, P], U8, align_bytes=64)
@@ -72,15 +67,27 @@ def tile_proto_metric_s_kernel(tc, x1, x2, out):
         def pass_cols(c):
             return slice(c * K_PASS, (c + 1) * K_PASS)
 
-        def sum_shots(t):
-            for s in range(1, SHOT):
-                for c in range(PASSES):
-                    so_far = x2_sb[:, t, 0, pass_cols(c)] if s == 1 else total[:, t, pass_cols(c)]
-                    nc.vector.tensor_tensor(
-                        out=total[:, t, pass_cols(c)], in0=so_far, in1=x2_sb[:, t, s, pass_cols(c)], op=ALU.add
-                    )
+        def load_queries(t):
+            nc.sync.dma_start(out=x1_sb[:, t * D : (t + 1) * D], in_=x1_rows[:, t * D : (t + 1) * D])
 
-        def prepare_queries(t):
+        def load_shots(t):
+            for c in range(PASSES):
+                nc.sync.dma_start(out=x2_sb[:, t, 0:2, pass_cols(c)], in_=x2_rows[t][:, 0:2, pass_cols(c)])
+            if t == 0:
+                load_queries(0)
+            for s in range(2, SHOT):
+                nc.sync.dma_start(out=x2_sb[:, t, s, :], in_=x2_rows[t][:, s, :])
+                if t == 0:
+                    load_queries(s - 1)
+
+        def add_shot(t, s):
+            for c in range(PASSES):
+                so_far = x2_sb[:, t, 0, pass_cols(c)] if s == 1 else total[:, t, pass_cols(c)]
+                nc.vector.tensor_tensor(
+                    out=total[:, t, pass_cols(c)], in0=so_far, in1=x2_sb[:, t, s, pass_cols(c)], op=ALU.add
+                )
+
+        def transpose_queries(t):
             nc.scalar.activation(
                 out=q_squares_tiles[:, t, :], in_=x1_tiles[:, t, :], func=ACT.Square,
                 accum_out=q_sq[:, t : t + 1],
@@ -90,45 +97,62 @@ def tile_proto_metric_s_kernel(tc, x1, x2, out):
                 for u in range(HALVES):
                     nc.tensor.transpose(out=q_t[:, c, u, :], in_=x1_words[:, t, c, u, :], identity=ident[:])
             nc.scalar.copy(out=q_grouped_words[:, t], in_=q_t[:].rearrange("p c u i -> p c i u"))
+
+        def quantise_queries(t):
             nc.vector.quantize_mx(
                 out=q_codes[:, t].rearrange("p c i -> p (c i)").bitcast(FP8X4),
                 scales=q_scales[:, t].rearrange("p c i -> p (c i)"),
                 in_=q_grouped_tiles[:, t, :],
             )
 
-        def prepare_protos(t, c):
+        def transpose_protos(t, c):
             p_t = psum.tile([P, HALVES, PAIR, P], F32)
             for u in range(HALVES):
                 for e in range(PAIR):
                     nc.tensor.transpose(
                         out=p_t[:, u, e, :], in_=total_features[:, t, c, u, :, e], identity=ident[:]
                     )
+            return p_t[:].rearrange("p u e j -> p j (u e)")
+
+        def copy_protos_on_scalar(t, c, p_t_grouped):
+            nc.scalar.activation(out=p_grouped[:, t, c], in_=p_t_grouped, func=ACT.Copy, scale=1.0 / SHOT)
+
+        def copy_protos_on_vector(t, c, p_t_grouped):
+            nc.vector.tensor_scalar_mul(out=p_grouped[:, t, c], in0=p_t_grouped, scalar1=1.0 / SHOT)
+
+        def square_protos(t, c):
             nc.scalar.activation(
-                out=p_grouped[:, t, c], in_=p_t[:].rearrange("p u e j -> p j (u e)"), func=ACT.Copy,
-                scale=1.0 / SHOT,
+                out=p_squares[:, t, pass_cols(c)], in_=total[:, t, pass_cols(c)], func=ACT.Square,
+                scale=1.0 / SHOT, accum_out=p_sq_parts[:, t, c : c + 1],
             )
+
+        def repeat_p_sq(t):
+            nc.scalar.activation(
+                out=p_sq_repeated[:, t, :], in_=p_sq_parts[:, t, 0:1].to_broadcast([P, P]), func=ACT.Identity,
+                bias=p_sq_parts[:, t, 1:2], scale=1.0,
+            )
+
+        def quantise_protos(t, c):
             nc.vector.quantize_mx(
                 out=p_codes[:, t, c, :].bitcast(FP8X4),
                 scales=p_scales[:, t, c, :],
                 in_=p_grouped[:, t, c].rearrange("p j f -> p (j f)"),
             )
 
-        def scores(t):
-            nc.scalar.activation(
-                out=p_squares[:, t, :], in_=total[:, t, :], func=ACT.Square,
-                scale=1.0 / SHOT, accum_out=p_sq[:, t : t + 1],
-            )
+        def transpose_p_sq(t):
             p_sq_rows = psum.tile([P, P], F32)
-            nc.tensor.transpose(
-                out=p_sq_rows[:], in_=p_sq[:, t : t + 1].to_broadcast([P, P]), identity=ident[:]
-            )
-            norms = keep.tile([P, Q_TILES, P], F32, name="norms%d" % t)
+            nc.tensor.transpose(out=p_sq_rows[:], in_=p_sq_repeated[:, t, :], identity=ident[:])
+            return p_sq_rows
+
+        def add_norms(t, p_sq_rows):
             nc.vector.tensor_tensor(
-                out=norms[:],
+                out=norms[:, t],
                 in0=p_sq_rows[:].unsqueeze(1).to_broadcast([P, Q_TILES, P]),
                 in1=q_sq[:].unsqueeze(2).to_broadcast([P, Q_TILES, P]),
                 op=ALU.add,
             )
+
+        def cross_term(t):
             cross = psum.tile([P, Q_TILES, P], F32)
             for i in range(Q_TILES):
                 for c in range(PASSES):
@@ -141,17 +165,51 @@ def tile_proto_metric_s_kernel(tc, x1, x2, out):
                         start=(c == 0),
                         stop=(c == PASSES - 1),
                     )
-            score = keep.tile([P, Q_TILES, P], F32, name="score%d" % t)
-            nc.vector.scalar_tensor_tensor(
-                out=score[:], in0=cross[:], scalar=2.0, in1=norms[:], op0=ALU.mult, op1=ALU.subtract
-            )
-            nc.sync.dma_start(out=out_rows[:, :, t * P : (t + 1) * P], in_=score[:])
+            return cross
 
-        for t in range(N_TILES):
-            sum_shots(t)
+        def finish(t, cross):
+            nc.vector.scalar_tensor_tensor(
+                out=score[:, t], in0=cross[:], scalar=2.0, in1=norms[:, t], op0=ALU.mult, op1=ALU.subtract
+            )
+            nc.sync.dma_start(out=out_rows[:, :, t * P : (t + 1) * P], in_=score[:, t])
+
+        with tc.manual_schedule():
+            for t in range(N_TILES):
+                load_shots(t)
+            make_identity(nc, ident[:])
+
+            for t in range(N_TILES):
+                for s in range(1, SHOT):
+                    add_shot(t, s)
+                    step = t * (SHOT - 1) + s - 1
+                    if step < Q_TILES:
+                        transpose_queries(step)
+                    if QUANT_LAG <= step < QUANT_LAG + Q_TILES:
+                        quantise_queries(step - QUANT_LAG)
+                if t == 0:
+                    first_banks = [transpose_protos(0, c) for c in range(PASSES)]
+                    for c in range(PASSES):
+                        copy_protos_on_scalar(0, c, first_banks[c])
+                    for c in range(PASSES):
+                        square_protos(0, c)
+                    repeat_p_sq(0)
+
+            bank_0 = transpose_protos(1, 0)
+            p_sq_rows_0 = transpose_p_sq(0)
+            bank_1 = transpose_protos(1, 1)
+            square_protos(1, 0)
+            copy_protos_on_scalar(1, 0, bank_0)
+            square_protos(1, 1)
+            repeat_p_sq(1)
             for c in range(PASSES):
-                prepare_protos(t, c)
-        for t in range(Q_TILES):
-            prepare_queries(t)
-        for t in range(N_TILES):
-            scores(t)
+                quantise_protos(0, c)
+            cross_0 = cross_term(0)
+            add_norms(0, p_sq_rows_0)
+            copy_protos_on_vector(1, 1, bank_1)
+            for c in range(PASSES):
+                quantise_protos(1, c)
+            p_sq_rows_1 = transpose_p_sq(1)
+            cross_1 = cross_term(1)
+            finish(0, cross_0)
+            add_norms(1, p_sq_rows_1)
+            finish(1, cross_1)

@@ -15,12 +15,15 @@ K_PASS = P * PACK
 
 B, N, SHOT, D = 512, 256, 5, 1024
 Q_TILES = B // P
-N_TILES = N // P
 PASSES = D // K_PASS
 HALVES = 2
 PAIR = 2
+RUN = PAIR * P
 
-QUANT_LAG = 2
+SUMMED = 3 * RUN
+GROUPS = [22, 22, 21, 21, 21, 21]
+GROUP_STARTS = [sum(GROUPS[:g]) for g in range(len(GROUPS))]
+GROUP_MAX = max(GROUPS)
 
 FLOPS = 2 * B * N * D
 
@@ -29,27 +32,36 @@ def tile_proto_metric_s_kernel(tc, x1, x2, out):
     nc = tc.nc
 
     x1_rows = x1.rearrange("(p t) d a b -> p (t d a b)", t=Q_TILES)
-    x2_rows = x2.rearrange("(t p) s d a b -> t p s (d a b)", p=P)
+    x2_shots = x2.rearrange("(t p) s d a b -> t p s (d a b)", p=P)
+    x2_rows = x2.rearrange("n s d a b -> (n s) (d a b)")
     out_rows = out.rearrange("(p t) j -> p t j", t=Q_TILES)
 
-    with tc.tile_pool(name="keep", bufs=1) as keep, tc.psum_pool(name="psum", bufs=2) as psum:
+    with tc.tile_pool(name="keep", bufs=1) as keep, tc.psum_pool(name="psum", bufs=1) as psum:
         x1_sb = keep.tile([P, Q_TILES * D], BF16)
-        x2_sb = keep.tile([P, N_TILES, SHOT, D], BF16)
+        shots_01 = [keep.tile([P, 2, K_PASS], BF16, name=f"shots_01_{c}") for c in range(PASSES)]
+        shots_24 = keep.tile([P, SHOT - 2, D], BF16)
+        shots_end = keep.tile([P, SHOT, RUN], BF16)
+        rows_sb = keep.tile([P, len(GROUPS), SUMMED], BF16)
         ident = keep.tile([P, P], F32)
-        total = keep.tile([P, N_TILES, D], F32)
+        chooser = keep.tile([P, GROUP_MAX], BF16)
+        total = keep.tile([P, PASSES, HALVES, PAIR, P], F32)
+        total_end = keep.tile([P, PAIR, P], F32)
         q_squares = keep.tile([P, Q_TILES * D], BF16)
-        p_squares = keep.tile([P, N_TILES, D], BF16)
+        p_squares = keep.tile([P, D], BF16)
+        p_squares_end = keep.tile([P, RUN], BF16)
+        squares = keep.tile([P, 3, PAIR, P], F32)
         q_sq = keep.tile([P, Q_TILES], F32)
-        p_sq_parts = keep.tile([P, N_TILES, PASSES], F32)
-        p_sq_repeated = keep.tile([P, N_TILES, P], F32)
-        norms = keep.tile([P, N_TILES, Q_TILES, P], F32)
-        score = keep.tile([P, N_TILES, Q_TILES, P], F32)
+        p_sq_last = keep.tile([P, 1], F32)
+        p_sq_end = keep.tile([P, 1], F32)
+        p_sq_summed = keep.tile([P, 1], F32)
+        p_sq_rows = keep.tile([P, N], F32)
+        score = keep.tile([P, Q_TILES, N], F32)
         q_grouped = keep.tile([P, Q_TILES * PASSES * P * PACK], BF16, align_bytes=64)
         q_codes = keep.tile([P, Q_TILES, PASSES, P], U32, align_bytes=64)
         q_scales = keep.tile([P, Q_TILES, PASSES, P], U8, align_bytes=64)
-        p_grouped = keep.tile([P, N_TILES, PASSES, P, PACK], BF16, align_bytes=64)
-        p_codes = keep.tile([P, N_TILES, PASSES, P], U32, align_bytes=64)
-        p_scales = keep.tile([P, N_TILES, PASSES, P], U8, align_bytes=64)
+        p_grouped = keep.tile([P, PASSES, N, PACK], BF16, align_bytes=64)
+        p_codes = keep.tile([P, PASSES, N], U32, align_bytes=64)
+        p_scales = keep.tile([P, PASSES, N], U8, align_bytes=64)
 
         x1_words = x1_sb[:].bitcast(F32).rearrange(
             "p (t c u w) -> p t c u w", t=Q_TILES, c=PASSES, u=HALVES
@@ -60,9 +72,9 @@ def tile_proto_metric_s_kernel(tc, x1, x2, out):
         q_grouped_tiles = q_grouped[:].rearrange("p (t k) -> p t k", t=Q_TILES)
         x1_tiles = x1_sb[:].rearrange("p (t d) -> p t d", t=Q_TILES)
         q_squares_tiles = q_squares[:].rearrange("p (t d) -> p t d", t=Q_TILES)
-        total_features = total[:].rearrange(
-            "p t (c u w e) -> p t c u w e", c=PASSES, u=HALVES, e=PAIR
-        )
+
+        def bank():
+            return psum.tile([P, HALVES, PAIR, P], F32, name="bank", bufs=6)
 
         def pass_cols(c):
             return slice(c * K_PASS, (c + 1) * K_PASS)
@@ -70,33 +82,86 @@ def tile_proto_metric_s_kernel(tc, x1, x2, out):
         def load_queries(t):
             nc.sync.dma_start(out=x1_sb[:, t * D : (t + 1) * D], in_=x1_rows[:, t * D : (t + 1) * D])
 
-        def load_shots(t):
-            for c in range(PASSES):
-                nc.sync.dma_start(out=x2_sb[:, t, 0:2, pass_cols(c)], in_=x2_rows[t][:, 0:2, pass_cols(c)])
-            if t == 0:
-                load_queries(0)
-            for s in range(2, SHOT):
-                nc.sync.dma_start(out=x2_sb[:, t, s, :], in_=x2_rows[t][:, s, :])
-                if t == 0:
-                    load_queries(s - 1)
+        def load_first_shots(c):
+            nc.sync.dma_start(out=shots_01[c][:], in_=x2_shots[1][:, 0:2, pass_cols(c)])
 
-        def add_shot(t, s):
-            for c in range(PASSES):
-                so_far = x2_sb[:, t, 0, pass_cols(c)] if s == 1 else total[:, t, pass_cols(c)]
-                nc.vector.tensor_tensor(
-                    out=total[:, t, pass_cols(c)], in0=so_far, in1=x2_sb[:, t, s, pass_cols(c)], op=ALU.add
-                )
+        def load_shot(s):
+            nc.sync.dma_start(out=shots_24[:, s - 2, :], in_=x2_shots[1][:, s, :])
 
-        def transpose_queries(t):
+        def load_end():
+            nc.sync.dma_start(out=shots_end[:], in_=x2_shots[0][:, :, SUMMED:D])
+
+        def load_rows(g):
+            r = SHOT * GROUP_STARTS[g]
+            nc.sync.dma_start(out=rows_sb[:, g, :], in_=x2_rows[r : r + P, 0:SUMMED])
+
+        def sorted_shot(s, c):
+            features = shots_01[c][:, s, :] if s < 2 else shots_24[:, s - 2, pass_cols(c)]
+            return features.rearrange("p (u w e) -> p u e w", u=HALVES, e=PAIR)
+
+        def add_shot(s, c):
+            so_far = sorted_shot(0, c) if s == 1 else total[:, c]
+            nc.vector.tensor_tensor(out=total[:, c], in0=so_far, in1=sorted_shot(s, c), op=ALU.add)
+
+        def sorted_end(s):
+            return shots_end[:, s, :].rearrange("p (w e) -> p e w", e=PAIR)
+
+        def add_end(s):
+            so_far = sorted_end(0) if s == 1 else total_end[:]
+            nc.vector.tensor_tensor(out=total_end[:], in0=so_far, in1=sorted_end(s), op=ALU.add)
+
+        def transpose_last(c):
+            p_t = bank()
+            for u in range(HALVES):
+                for e in range(PAIR):
+                    nc.tensor.transpose(out=p_t[:, u, e, :], in_=total[:, c, u, e, :], identity=ident[:])
+            return p_t
+
+        def transpose_end(p_t):
+            for e in range(PAIR):
+                nc.tensor.transpose(out=p_t[:, 1, e, :], in_=total_end[:, e, :], identity=ident[:])
+
+        def sum_rows(g, banks):
+            n0, n = GROUP_STARTS[g], GROUPS[g]
+            run_cols = rows_sb[:, g, :].rearrange("p (r w e) -> p r e w", r=3, e=PAIR)
+            for r in range(3):
+                for e in range(PAIR):
+                    nc.tensor.matmul(
+                        out=banks[r // 2][:, r % 2, e, n0 : n0 + n], lhsT=run_cols[:, r, e, :],
+                        rhs=chooser[:, 0:n], start=True, stop=True,
+                    )
+
+        def copy_protos(engine, half, c, p_t):
+            dst = p_grouped[:, c, half * P : (half + 1) * P, :]
+            src = p_t[:].rearrange("p u e j -> p j (u e)")
+            if engine == "vector":
+                nc.vector.tensor_scalar_mul(out=dst, in0=src, scalar1=2.0 / SHOT)
+            else:
+                nc.scalar.activation(out=dst, in_=src, func=ACT.Copy, scale=2.0 / SHOT)
+
+        def quantise_protos(half, c):
+            cols = slice(half * P, (half + 1) * P)
+            nc.vector.quantize_mx(
+                out=p_codes[:, c, cols].bitcast(FP8X4),
+                scales=p_scales[:, c, cols],
+                in_=p_grouped[:, c, cols, :].rearrange("p j f -> p (j f)"),
+            )
+
+        def square_queries(t):
             nc.scalar.activation(
                 out=q_squares_tiles[:, t, :], in_=x1_tiles[:, t, :], func=ACT.Square,
                 accum_out=q_sq[:, t : t + 1],
             )
-            q_t = psum.tile([P, PASSES, HALVES, P], F32)
+
+        def transpose_queries(t):
+            q_t = bank()
             for c in range(PASSES):
                 for u in range(HALVES):
                     nc.tensor.transpose(out=q_t[:, c, u, :], in_=x1_words[:, t, c, u, :], identity=ident[:])
-            nc.scalar.copy(out=q_grouped_words[:, t], in_=q_t[:].rearrange("p c u i -> p c i u"))
+            return q_t
+
+        def copy_queries(engine_copy, t, q_t):
+            engine_copy(out=q_grouped_words[:, t], in_=q_t[:].rearrange("p c u i -> p c i u"))
 
         def quantise_queries(t):
             nc.vector.quantize_mx(
@@ -105,111 +170,145 @@ def tile_proto_metric_s_kernel(tc, x1, x2, out):
                 in_=q_grouped_tiles[:, t, :],
             )
 
-        def transpose_protos(t, c):
-            p_t = psum.tile([P, HALVES, PAIR, P], F32)
-            for u in range(HALVES):
+        def square_last():
+            nc.scalar.activation(
+                out=p_squares[:], in_=total[:].rearrange("p c u e w -> p (c u e w)"), func=ACT.Square,
+                scale=1.0 / SHOT, accum_out=p_sq_last[:],
+            )
+
+        def square_end():
+            nc.scalar.activation(
+                out=p_squares_end[:], in_=total_end[:].rearrange("p e w -> p (e w)"), func=ACT.Square,
+                scale=1.0 / SHOT, accum_out=p_sq_end[:],
+            )
+
+        def square_summed(c, p_t):
+            runs = HALVES - c
+            nc.scalar.activation(
+                out=squares[:, 2 * c : 2 * c + runs], in_=p_t[:, 0:runs], func=ACT.Square, scale=1.0 / SHOT
+            )
+
+        def transpose_squares(p_sq_t):
+            for r in range(3):
                 for e in range(PAIR):
-                    nc.tensor.transpose(
-                        out=p_t[:, u, e, :], in_=total_features[:, t, c, u, :, e], identity=ident[:]
+                    nc.tensor.matmul(
+                        out=p_sq_t[:, 0, 0, :], lhsT=squares[:, r, e, :], rhs=ident[:],
+                        start=(r + e == 0), stop=(r + e == 3), is_transpose=True,
                     )
-            return p_t[:].rearrange("p u e j -> p j (u e)")
 
-        def copy_protos_on_scalar(t, c, p_t_grouped):
-            nc.scalar.activation(out=p_grouped[:, t, c], in_=p_t_grouped, func=ACT.Copy, scale=1.0 / SHOT)
-
-        def copy_protos_on_vector(t, c, p_t_grouped):
-            nc.vector.tensor_scalar_mul(out=p_grouped[:, t, c], in0=p_t_grouped, scalar1=1.0 / SHOT)
-
-        def square_protos(t, c):
-            nc.scalar.activation(
-                out=p_squares[:, t, pass_cols(c)], in_=total[:, t, pass_cols(c)], func=ACT.Square,
-                scale=1.0 / SHOT, accum_out=p_sq_parts[:, t, c : c + 1],
+        def reduce_squares(p_sq_t):
+            nc.vector.tensor_reduce(
+                out=p_sq_summed[:], in_=p_sq_t[:, 0, 0, :], axis=mybir.AxisListType.X, op=ALU.add
             )
 
-        def repeat_p_sq(t):
-            nc.scalar.activation(
-                out=p_sq_repeated[:, t, :], in_=p_sq_parts[:, t, 0:1].to_broadcast([P, P]), func=ACT.Identity,
-                bias=p_sq_parts[:, t, 1:2], scale=1.0,
-            )
+        def spread(dst, parts):
+            for k, part in enumerate(parts):
+                nc.tensor.matmul(
+                    out=dst, lhsT=part[:].to_broadcast([P, P]), rhs=ident[:],
+                    start=(k == 0), stop=(k == len(parts) - 1), is_transpose=True,
+                )
 
-        def quantise_protos(t, c):
-            nc.vector.quantize_mx(
-                out=p_codes[:, t, c, :].bitcast(FP8X4),
-                scales=p_scales[:, t, c, :],
-                in_=p_grouped[:, t, c].rearrange("p j f -> p (j f)"),
-            )
+        def cross_term(i, cross):
+            for c in range(PASSES):
+                nc.tensor.matmul_mx(
+                    out=cross[:, i % 2, :],
+                    lhsT=q_codes[:, i, c, :].bitcast(FP8X4),
+                    lhsT_scale=q_scales[:, i, c, :],
+                    rhs=p_codes[:, c, :].bitcast(FP8X4),
+                    rhs_scale=p_scales[:, c, :],
+                    start=(c == 0),
+                    stop=(c == PASSES - 1),
+                )
 
-        def transpose_p_sq(t):
-            p_sq_rows = psum.tile([P, P], F32)
-            nc.tensor.transpose(out=p_sq_rows[:], in_=p_sq_repeated[:, t, :], identity=ident[:])
-            return p_sq_rows
-
-        def add_norms(t, p_sq_rows):
-            nc.vector.tensor_tensor(
-                out=norms[:, t],
-                in0=p_sq_rows[:].unsqueeze(1).to_broadcast([P, Q_TILES, P]),
-                in1=q_sq[:].unsqueeze(2).to_broadcast([P, Q_TILES, P]),
-                op=ALU.add,
-            )
-
-        def cross_term(t):
-            cross = psum.tile([P, Q_TILES, P], F32)
-            for i in range(Q_TILES):
-                for c in range(PASSES):
-                    nc.tensor.matmul_mx(
-                        out=cross[:, i, :],
-                        lhsT=q_codes[:, i, c, :].bitcast(FP8X4),
-                        lhsT_scale=q_scales[:, i, c, :],
-                        rhs=p_codes[:, t, c, :].bitcast(FP8X4),
-                        rhs_scale=p_scales[:, t, c, :],
-                        start=(c == 0),
-                        stop=(c == PASSES - 1),
-                    )
-            return cross
-
-        def finish(t, cross):
+        def finish(i, cross):
             nc.vector.scalar_tensor_tensor(
-                out=score[:, t], in0=cross[:], scalar=2.0, in1=norms[:, t], op0=ALU.mult, op1=ALU.subtract
+                out=score[:, i, :], in0=cross[:, i % 2, :], scalar=q_sq[:, i : i + 1], in1=p_sq_rows[:],
+                op0=ALU.subtract, op1=ALU.subtract,
             )
-            nc.sync.dma_start(out=out_rows[:, :, t * P : (t + 1) * P], in_=score[:, t])
+            nc.sync.dma_start(out=out_rows[:, i, :], in_=score[:, i, :])
+
+        def make_chooser():
+            nc.gpsimd.memset(chooser[:], 1.0)
+            nc.gpsimd.affine_select(
+                out=chooser[:], in_=chooser[:], pattern=[[-SHOT, GROUP_MAX]], compare_op=ALU.is_ge,
+                fill=0.0, base=0, channel_multiplier=1,
+            )
+            nc.gpsimd.affine_select(
+                out=chooser[:], in_=chooser[:], pattern=[[SHOT, GROUP_MAX]], compare_op=ALU.is_ge,
+                fill=0.0, base=SHOT - 1, channel_multiplier=-1,
+            )
 
         with tc.manual_schedule():
-            for t in range(N_TILES):
-                load_shots(t)
+            load_first_shots(0)
+            load_queries(0)
+            load_first_shots(1)
+            load_shot(2)
+            load_shot(3)
+            load_end()
+            load_queries(1)
+            load_shot(4)
+            load_queries(2)
+            for g in range(len(GROUPS)):
+                load_rows(g)
+            load_queries(3)
             make_identity(nc, ident[:])
+            make_chooser()
+            crosses = [psum.tile([P, 2, N], F32, name=f"cross_{k}") for k in range(2)]
 
-            for t in range(N_TILES):
-                for s in range(1, SHOT):
-                    add_shot(t, s)
-                    step = t * (SHOT - 1) + s - 1
-                    if step < Q_TILES:
-                        transpose_queries(step)
-                    if QUANT_LAG <= step < QUANT_LAG + Q_TILES:
-                        quantise_queries(step - QUANT_LAG)
-                if t == 0:
-                    first_banks = [transpose_protos(0, c) for c in range(PASSES)]
-                    for c in range(PASSES):
-                        copy_protos_on_scalar(0, c, first_banks[c])
-                    for c in range(PASSES):
-                        square_protos(0, c)
-                    repeat_p_sq(0)
-
-            bank_0 = transpose_protos(1, 0)
-            p_sq_rows_0 = transpose_p_sq(0)
-            bank_1 = transpose_protos(1, 1)
-            square_protos(1, 0)
-            copy_protos_on_scalar(1, 0, bank_0)
-            square_protos(1, 1)
-            repeat_p_sq(1)
             for c in range(PASSES):
-                quantise_protos(0, c)
-            cross_0 = cross_term(0)
-            add_norms(0, p_sq_rows_0)
-            copy_protos_on_vector(1, 1, bank_1)
+                add_shot(1, c)
+            square_queries(0)
+            q_t = transpose_queries(0)
+            copy_queries(nc.scalar.copy, 0, q_t)
             for c in range(PASSES):
-                quantise_protos(1, c)
-            p_sq_rows_1 = transpose_p_sq(1)
-            cross_1 = cross_term(1)
-            finish(0, cross_0)
-            add_norms(1, p_sq_rows_1)
-            finish(1, cross_1)
+                add_shot(2, c)
+            for c in range(PASSES):
+                add_shot(3, c)
+            quantise_queries(0)
+            add_end(1)
+            square_queries(1)
+            q_t = transpose_queries(1)
+            copy_queries(nc.scalar.copy, 1, q_t)
+            add_shot(4, 0)
+            add_end(2)
+            add_shot(4, 1)
+            add_end(3)
+            square_queries(2)
+            q_t = transpose_queries(2)
+            copy_queries(nc.scalar.copy, 2, q_t)
+            last_0 = transpose_last(0)
+            last_1 = transpose_last(1)
+            quantise_queries(1)
+            add_end(4)
+            copy_protos("vector", 1, 0, last_0)
+            square_last()
+            copy_protos("vector", 1, 1, last_1)
+            first = [bank(), bank()]
+            for g in range(len(GROUPS)):
+                sum_rows(g, first)
+            transpose_end(first[1])
+            q_t = transpose_queries(3)
+            p_sq_t = bank()
+            quantise_queries(2)
+            quantise_protos(1, 0)
+            square_summed(0, first[0])
+            copy_protos("vector", 0, 1, first[1])
+            quantise_protos(1, 1)
+            square_summed(1, first[1])
+            transpose_squares(p_sq_t)
+            copy_protos("vector", 0, 0, first[0])
+            quantise_protos(0, 1)
+            copy_queries(nc.scalar.copy, 3, q_t)
+            quantise_protos(0, 0)
+            square_end()
+            reduce_squares(p_sq_t)
+            square_queries(3)
+            rows = bank()
+            spread(rows[:, 0, 1, :], [p_sq_last])
+            spread(rows[:, 0, 0, :], [p_sq_end, p_sq_summed])
+            quantise_queries(3)
+            nc.vector.tensor_copy(out=p_sq_rows[:], in_=rows[:, 0].rearrange("p t j -> p (t j)"))
+            for i in range(Q_TILES):
+                cross_term(i, crosses[i // 2])
+            for i in range(Q_TILES):
+                finish(i, crosses[i // 2])

@@ -239,76 +239,87 @@ def tile_proto_metric_s_kernel(tc, x1, x2, out):
             )
 
         with tc.manual_schedule():
-            load_first_shots(0)
-            load_queries(0)
-            load_first_shots(1)
-            load_shot(2)
-            load_shot(3)
-            load_end()
-            load_queries(1)
-            load_shot(4)
-            load_queries(2)
-            for g in range(len(GROUPS)):
-                load_rows(g)
-            load_queries(3)
             make_identity(nc, ident[:])
             make_chooser()
             crosses = [psum.tile([P, 2, N], F32, name=f"cross_{k}") for k in range(2)]
-
-            for c in range(PASSES):
-                add_shot(1, c)
+            load_first_shots(0)
+            load_first_shots(1)
+            load_shot(2)
+            load_shot(3)
+            load_queries(0)
+            load_shot(4)
+            load_rows(0)
+            load_end()
+            load_rows(1)
+            load_rows(2)
+            load_rows(3)
+            load_rows(4)
+            load_rows(5)
+            load_queries(1)
+            load_queries(2)
+            load_queries(3)
+            q_t0 = transpose_queries(0)
+            first = [bank(), bank()]
+            sum_rows(0, first)
             square_queries(0)
-            q_t = transpose_queries(0)
-            copy_queries(nc.scalar.copy, 0, q_t)
-            for c in range(PASSES):
-                add_shot(2, c)
-            for c in range(PASSES):
-                add_shot(3, c)
-            quantise_queries(0)
-            add_end(1)
-            square_queries(1)
-            q_t = transpose_queries(1)
-            copy_queries(nc.scalar.copy, 1, q_t)
+            copy_queries(nc.scalar.copy, 0, q_t0)
+            add_shot(1, 0)
+            add_shot(1, 1)
+            add_shot(2, 0)
+            add_shot(2, 1)
+            add_shot(3, 0)
+            add_shot(3, 1)
             add_shot(4, 0)
-            add_end(2)
             add_shot(4, 1)
-            add_end(3)
-            square_queries(2)
-            q_t = transpose_queries(2)
-            copy_queries(nc.scalar.copy, 2, q_t)
+            add_end(1)
+            quantise_queries(0)
+            add_end(2)
             last_0 = transpose_last(0)
             last_1 = transpose_last(1)
-            quantise_queries(1)
-            add_end(4)
-            copy_protos("vector", 1, 0, last_0)
+            sum_rows(1, first)
+            sum_rows(2, first)
+            sum_rows(3, first)
+            sum_rows(4, first)
+            sum_rows(5, first)
             square_last()
-            copy_protos("vector", 1, 1, last_1)
-            first = [bank(), bank()]
-            for g in range(len(GROUPS)):
-                sum_rows(g, first)
-            transpose_end(first[1])
-            q_t = transpose_queries(3)
-            p_sq_t = bank()
-            quantise_queries(2)
-            quantise_protos(1, 0)
-            square_summed(0, first[0])
-            copy_protos("vector", 0, 1, first[1])
-            quantise_protos(1, 1)
-            square_summed(1, first[1])
-            transpose_squares(p_sq_t)
+            copy_protos("scalar", 1, 1, last_1)
+            copy_protos("vector", 1, 0, last_0)
+            add_end(3)
+            add_end(4)
             copy_protos("vector", 0, 0, first[0])
-            quantise_protos(0, 1)
-            copy_queries(nc.scalar.copy, 3, q_t)
-            quantise_protos(0, 0)
+            quantise_protos(1, 0)
+            transpose_end(first[1])
+            q_t1 = transpose_queries(1)
+            q_t2 = transpose_queries(2)
             square_end()
-            reduce_squares(p_sq_t)
+            square_summed(0, first[0])
+            square_summed(1, first[1])
+            copy_queries(nc.scalar.copy, 1, q_t1)
+            square_queries(1)
+            square_queries(2)
             square_queries(3)
+            copy_protos("vector", 0, 1, first[1])
+            quantise_protos(0, 0)
+            quantise_protos(1, 1)
+            quantise_protos(0, 1)
+            copy_queries(nc.vector.tensor_copy, 2, q_t2)
+            p_sq_t = bank()
+            transpose_squares(p_sq_t)
+            q_t3 = transpose_queries(3)
+            reduce_squares(p_sq_t)
+            quantise_queries(1)
+            copy_queries(nc.vector.tensor_copy, 3, q_t3)
+            quantise_queries(2)
             rows = bank()
             spread(rows[:, 0, 1, :], [p_sq_last])
             spread(rows[:, 0, 0, :], [p_sq_end, p_sq_summed])
-            quantise_queries(3)
+            cross_term(0, crosses[0])
+            cross_term(1, crosses[0])
+            cross_term(2, crosses[1])
             nc.vector.tensor_copy(out=p_sq_rows[:], in_=rows[:, 0].rearrange("p t j -> p (t j)"))
-            for i in range(Q_TILES):
-                cross_term(i, crosses[i // 2])
-            for i in range(Q_TILES):
-                finish(i, crosses[i // 2])
+            quantise_queries(3)
+            finish(0, crosses[0])
+            finish(1, crosses[0])
+            finish(2, crosses[1])
+            cross_term(3, crosses[1])
+            finish(3, crosses[1])

@@ -21,7 +21,8 @@ PAIR = 2
 RUN = PAIR * P
 
 SUMMED = 3 * RUN
-GROUPS = [22, 22, 21, 21, 21, 21]
+GROUPS = [25, 25, 25, 25, 25, 3]
+FEW_ROWS = 16
 GROUP_STARTS = [sum(GROUPS[:g]) for g in range(len(GROUPS))]
 GROUP_MAX = max(GROUPS)
 
@@ -41,7 +42,8 @@ def tile_proto_metric_s_kernel(tc, x1, x2, out):
         shots_01 = [keep.tile([P, 2, K_PASS], BF16, name=f"shots_01_{c}") for c in range(PASSES)]
         shots_24 = keep.tile([P, SHOT - 2, D], BF16)
         shots_end = keep.tile([P, SHOT, RUN], BF16)
-        rows_sb = keep.tile([P, len(GROUPS), SUMMED], BF16)
+        rows_sb = [keep.tile([P, SUMMED], BF16, name=f"rows_{g}") for g in range(len(GROUPS))]
+        rows_few = rows_sb[-1]
         ident = keep.tile([P, P], F32)
         chooser = keep.tile([P, GROUP_MAX], BF16)
         total = keep.tile([P, PASSES, HALVES, PAIR, P], F32)
@@ -74,7 +76,7 @@ def tile_proto_metric_s_kernel(tc, x1, x2, out):
         q_squares_tiles = q_squares[:].rearrange("p (t d) -> p t d", t=Q_TILES)
 
         def bank():
-            return psum.tile([P, HALVES, PAIR, P], F32, name="bank", bufs=6)
+            return psum.tile([P, HALVES, PAIR, P], F32, name="bank", bufs=8)
 
         def pass_cols(c):
             return slice(c * K_PASS, (c + 1) * K_PASS)
@@ -93,7 +95,8 @@ def tile_proto_metric_s_kernel(tc, x1, x2, out):
 
         def load_rows(g):
             r = SHOT * GROUP_STARTS[g]
-            nc.sync.dma_start(out=rows_sb[:, g, :], in_=x2_rows[r : r + P, 0:SUMMED])
+            rows = FEW_ROWS if g == len(GROUPS) - 1 else P
+            nc.sync.dma_start(out=rows_sb[g][0:rows, :], in_=x2_rows[r : r + rows, 0:SUMMED])
 
         def sorted_shot(s, c):
             features = shots_01[c][:, s, :] if s < 2 else shots_24[:, s - 2, pass_cols(c)]
@@ -123,7 +126,7 @@ def tile_proto_metric_s_kernel(tc, x1, x2, out):
 
         def sum_rows(g, banks):
             n0, n = GROUP_STARTS[g], GROUPS[g]
-            run_cols = rows_sb[:, g, :].rearrange("p (r w e) -> p r e w", r=3, e=PAIR)
+            run_cols = rows_sb[g][:].rearrange("p (r w e) -> p r e w", r=3, e=PAIR)
             for r in range(3):
                 for e in range(PAIR):
                     nc.tensor.matmul(
@@ -208,10 +211,12 @@ def tile_proto_metric_s_kernel(tc, x1, x2, out):
                     start=(k == 0), stop=(k == len(parts) - 1), is_transpose=True,
                 )
 
-        def cross_term(i, cross):
+        def cross_term(i):
+            tile = bank()
+            cross = tile[:].rearrange("p u e j -> p (u e j)")[:, 0:N]
             for c in range(PASSES):
                 nc.tensor.matmul_mx(
-                    out=cross[:, i % 2, :],
+                    out=cross,
                     lhsT=q_codes[:, i, c, :].bitcast(FP8X4),
                     lhsT_scale=q_scales[:, i, c, :],
                     rhs=p_codes[:, c, :].bitcast(FP8X4),
@@ -219,10 +224,11 @@ def tile_proto_metric_s_kernel(tc, x1, x2, out):
                     start=(c == 0),
                     stop=(c == PASSES - 1),
                 )
+            return cross
 
         def finish(i, cross):
             nc.vector.scalar_tensor_tensor(
-                out=score[:, i, :], in0=cross[:, i % 2, :], scalar=q_sq[:, i : i + 1], in1=p_sq_rows[:],
+                out=score[:, i, :], in0=cross, scalar=q_sq[:, i : i + 1], in1=p_sq_rows[:],
                 op0=ALU.subtract, op1=ALU.subtract,
             )
             nc.sync.dma_start(out=out_rows[:, i, :], in_=score[:, i, :])
@@ -241,28 +247,29 @@ def tile_proto_metric_s_kernel(tc, x1, x2, out):
         with tc.manual_schedule():
             make_identity(nc, ident[:])
             make_chooser()
-            crosses = [psum.tile([P, 2, N], F32, name=f"cross_{k}") for k in range(2)]
+            nc.vector.memset(rows_few[:], 0.0)
             load_first_shots(0)
             load_first_shots(1)
             load_shot(2)
             load_shot(3)
             load_queries(0)
             load_shot(4)
+            load_rows(5)
             load_rows(0)
             load_end()
             load_rows(1)
             load_rows(2)
             load_rows(3)
             load_rows(4)
-            load_rows(5)
             load_queries(1)
             load_queries(2)
             load_queries(3)
             q_t0 = transpose_queries(0)
             first = [bank(), bank()]
+            sum_rows(5, first)
             sum_rows(0, first)
-            square_queries(0)
             copy_queries(nc.scalar.copy, 0, q_t0)
+            square_queries(0)
             add_shot(1, 0)
             add_shot(1, 1)
             add_shot(2, 0)
@@ -271,55 +278,54 @@ def tile_proto_metric_s_kernel(tc, x1, x2, out):
             add_shot(3, 1)
             add_shot(4, 0)
             add_shot(4, 1)
-            add_end(1)
             quantise_queries(0)
-            add_end(2)
+            add_end(1)
             last_0 = transpose_last(0)
             last_1 = transpose_last(1)
             sum_rows(1, first)
             sum_rows(2, first)
             sum_rows(3, first)
             sum_rows(4, first)
-            sum_rows(5, first)
             square_last()
             copy_protos("scalar", 1, 1, last_1)
             copy_protos("vector", 1, 0, last_0)
+            add_end(2)
+            quantise_protos(1, 0)
             add_end(3)
             add_end(4)
             copy_protos("vector", 0, 0, first[0])
-            quantise_protos(1, 0)
+            quantise_protos(0, 0)
             transpose_end(first[1])
             q_t1 = transpose_queries(1)
             q_t2 = transpose_queries(2)
             square_end()
-            square_summed(0, first[0])
             square_summed(1, first[1])
+            square_summed(0, first[0])
             copy_queries(nc.scalar.copy, 1, q_t1)
             square_queries(1)
             square_queries(2)
             square_queries(3)
             copy_protos("vector", 0, 1, first[1])
-            quantise_protos(0, 0)
             quantise_protos(1, 1)
-            quantise_protos(0, 1)
             copy_queries(nc.vector.tensor_copy, 2, q_t2)
+            quantise_protos(0, 1)
+            quantise_queries(1)
             p_sq_t = bank()
             transpose_squares(p_sq_t)
             q_t3 = transpose_queries(3)
             reduce_squares(p_sq_t)
-            quantise_queries(1)
-            copy_queries(nc.vector.tensor_copy, 3, q_t3)
             quantise_queries(2)
+            copy_queries(nc.vector.tensor_copy, 3, q_t3)
             rows = bank()
             spread(rows[:, 0, 1, :], [p_sq_last])
             spread(rows[:, 0, 0, :], [p_sq_end, p_sq_summed])
-            cross_term(0, crosses[0])
-            cross_term(1, crosses[0])
-            cross_term(2, crosses[1])
+            cross_0 = cross_term(0)
+            cross_1 = cross_term(1)
+            cross_2 = cross_term(2)
             nc.vector.tensor_copy(out=p_sq_rows[:], in_=rows[:, 0].rearrange("p t j -> p (t j)"))
             quantise_queries(3)
-            finish(0, crosses[0])
-            finish(1, crosses[0])
-            finish(2, crosses[1])
-            cross_term(3, crosses[1])
-            finish(3, crosses[1])
+            finish(0, cross_0)
+            finish(1, cross_1)
+            finish(2, cross_2)
+            cross_3 = cross_term(3)
+            finish(3, cross_3)

@@ -211,27 +211,30 @@ def tile_proto_metric_s_kernel(tc, x1, x2, out):
                     start=(k == 0), stop=(k == len(parts) - 1), is_transpose=True,
                 )
 
-        def cross_term(i):
+        def load_query_pair():
+            nc.sync.dma_start(out=x1_sb[:, 2 * D :], in_=x1_rows[:, 2 * D :])
+
+        def cross_term(i, j0=0, j1=N):
             tile = bank()
-            cross = tile[:].rearrange("p u e j -> p (u e j)")[:, 0:N]
+            cross = tile[:].rearrange("p u e j -> p (u e j)")[:, 0 : j1 - j0]
             for c in range(PASSES):
                 nc.tensor.matmul_mx(
                     out=cross,
                     lhsT=q_codes[:, i, c, :].bitcast(FP8X4),
                     lhsT_scale=q_scales[:, i, c, :],
-                    rhs=p_codes[:, c, :].bitcast(FP8X4),
-                    rhs_scale=p_scales[:, c, :],
+                    rhs=p_codes[:, c, j0:j1].bitcast(FP8X4),
+                    rhs_scale=p_scales[:, c, j0:j1],
                     start=(c == 0),
                     stop=(c == PASSES - 1),
                 )
             return cross
 
-        def finish(i, cross):
+        def finish(i, cross, j0=0, j1=N):
             nc.vector.scalar_tensor_tensor(
-                out=score[:, i, :], in0=cross, scalar=q_sq[:, i : i + 1], in1=p_sq_rows[:],
+                out=score[:, i, j0:j1], in0=cross, scalar=q_sq[:, i : i + 1], in1=p_sq_rows[:, j0:j1],
                 op0=ALU.subtract, op1=ALU.subtract,
             )
-            nc.sync.dma_start(out=out_rows[:, i, :], in_=score[:, i, :])
+            nc.sync.dma_start(out=out_rows[:, i, j0:j1], in_=score[:, i, j0:j1])
 
         def make_chooser():
             nc.gpsimd.memset(chooser[:], 1.0)
@@ -278,8 +281,9 @@ def tile_proto_metric_s_kernel(tc, x1, x2, out):
             add_shot(3, 1)
             add_shot(4, 0)
             add_shot(4, 1)
-            quantise_queries(0)
             add_end(1)
+            quantise_queries(0)
+            add_end(2)
             last_0 = transpose_last(0)
             last_1 = transpose_last(1)
             sum_rows(1, first)
@@ -289,13 +293,14 @@ def tile_proto_metric_s_kernel(tc, x1, x2, out):
             square_last()
             copy_protos("scalar", 1, 1, last_1)
             copy_protos("vector", 1, 0, last_0)
-            add_end(2)
-            quantise_protos(1, 0)
             add_end(3)
+            quantise_protos(1, 0)
             add_end(4)
             copy_protos("vector", 0, 0, first[0])
             quantise_protos(0, 0)
             transpose_end(first[1])
+            rows = bank()
+            spread(rows[:, 0, 1, :], [p_sq_last])
             q_t1 = transpose_queries(1)
             q_t2 = transpose_queries(2)
             square_end()
@@ -316,8 +321,6 @@ def tile_proto_metric_s_kernel(tc, x1, x2, out):
             reduce_squares(p_sq_t)
             quantise_queries(2)
             copy_queries(nc.vector.tensor_copy, 3, q_t3)
-            rows = bank()
-            spread(rows[:, 0, 1, :], [p_sq_last])
             spread(rows[:, 0, 0, :], [p_sq_end, p_sq_summed])
             cross_0 = cross_term(0)
             cross_1 = cross_term(1)
@@ -327,5 +330,7 @@ def tile_proto_metric_s_kernel(tc, x1, x2, out):
             finish(0, cross_0)
             finish(1, cross_1)
             finish(2, cross_2)
-            cross_3 = cross_term(3)
-            finish(3, cross_3)
+            cross_3a = cross_term(3, P, N)
+            cross_3b = cross_term(3, 0, P)
+            finish(3, cross_3a, P, N)
+            finish(3, cross_3b, 0, P)

@@ -46,7 +46,7 @@ def tile_proto_metric_s_kernel(tc, x1, x2, out):
         rows_few = rows_sb[-1]
         ident = keep.tile([P, P], F32)
         chooser = keep.tile([P, GROUP_MAX], BF16)
-        total = keep.tile([P, PASSES, HALVES, PAIR, P], F32)
+        total = keep.tile([P, D], F32)
         total_end = keep.tile([P, PAIR, P], F32)
         q_squares = keep.tile([P, Q_TILES * D], BF16)
         p_squares = keep.tile([P, D], BF16)
@@ -56,12 +56,14 @@ def tile_proto_metric_s_kernel(tc, x1, x2, out):
         p_sq_last = keep.tile([P, 1], F32)
         p_sq_end = keep.tile([P, 1], F32)
         p_sq_summed = keep.tile([P, 1], F32)
+        p_sq_parts = keep.tile([P, P], F32)
         p_sq_rows = keep.tile([P, N], F32)
         score = keep.tile([P, Q_TILES, N], F32)
         q_grouped = keep.tile([P, Q_TILES * PASSES * P * PACK], BF16, align_bytes=64)
         q_codes = keep.tile([P, Q_TILES, PASSES, P], U32, align_bytes=64)
         q_scales = keep.tile([P, Q_TILES, PASSES, P], U8, align_bytes=64)
         p_grouped = keep.tile([P, PASSES, N, PACK], BF16, align_bytes=64)
+        means = keep.tile([P, D], BF16)
         p_codes = keep.tile([P, PASSES, N], U32, align_bytes=64)
         p_scales = keep.tile([P, PASSES, N], U8, align_bytes=64)
 
@@ -76,7 +78,25 @@ def tile_proto_metric_s_kernel(tc, x1, x2, out):
         q_squares_tiles = q_squares[:].rearrange("p (t d) -> p t d", t=Q_TILES)
 
         def bank():
-            return psum.tile([P, HALVES, PAIR, P], F32, name="bank", bufs=8)
+            return psum.tile([P, HALVES, PAIR, P], F32, name="bank", bufs=7)
+
+        idle_in = keep.tile([P, PACK * N], BF16, align_bytes=64)
+        idle_codes = keep.tile([P, N], U32, align_bytes=64)
+        idle_scales = keep.tile([P, N], U8, align_bytes=64)
+        idle_bank = psum.tile([P, N], F32, name="idle_bank", bufs=1)
+
+        def quantise_idle():
+            nc.vector.memset(idle_in[:], 0.0)
+            nc.vector.quantize_mx(
+                out=idle_codes[:].bitcast(FP8X4), scales=idle_scales[:], in_=idle_in[:]
+            )
+
+        def warm_up(times):
+            for k in range(times):
+                nc.tensor.matmul_mx(
+                    out=idle_bank[:], lhsT=idle_codes[:, 0:P].bitcast(FP8X4), lhsT_scale=idle_scales[:, 0:P],
+                    rhs=idle_codes[:].bitcast(FP8X4), rhs_scale=idle_scales[:], start=True, stop=True,
+                )
 
         def pass_cols(c):
             return slice(c * K_PASS, (c + 1) * K_PASS)
@@ -98,13 +118,19 @@ def tile_proto_metric_s_kernel(tc, x1, x2, out):
             rows = FEW_ROWS if g == len(GROUPS) - 1 else P
             nc.sync.dma_start(out=rows_sb[g][0:rows, :], in_=x2_rows[r : r + rows, 0:SUMMED])
 
-        def sorted_shot(s, c):
-            features = shots_01[c][:, s, :] if s < 2 else shots_24[:, s - 2, pass_cols(c)]
-            return features.rearrange("p (u w e) -> p u e w", u=HALVES, e=PAIR)
+        def shot_part(s, c):
+            return shots_01[c][:, s, :] if s < 2 else shots_24[:, s - 2, pass_cols(c)]
 
         def add_shot(s, c):
-            so_far = sorted_shot(0, c) if s == 1 else total[:, c]
-            nc.vector.tensor_tensor(out=total[:, c], in0=so_far, in1=sorted_shot(s, c), op=ALU.add)
+            part = total[:, pass_cols(c)]
+            so_far = shot_part(0, c) if s == 1 else part
+            nc.vector.tensor_tensor(out=part, in0=so_far, in1=shot_part(s, c), op=ALU.add)
+
+        def add_whole_shot(s):
+            nc.vector.tensor_tensor(out=total[:], in0=total[:], in1=shots_24[:, s - 2, :], op=ALU.add)
+
+        def round_means(c):
+            nc.vector.tensor_scalar_mul(out=means[:, pass_cols(c)], in0=total[:, pass_cols(c)], scalar1=2.0 / SHOT)
 
         def sorted_end(s):
             return shots_end[:, s, :].rearrange("p (w e) -> p e w", e=PAIR)
@@ -113,12 +139,15 @@ def tile_proto_metric_s_kernel(tc, x1, x2, out):
             so_far = sorted_end(0) if s == 1 else total_end[:]
             nc.vector.tensor_tensor(out=total_end[:], in0=so_far, in1=sorted_end(s), op=ALU.add)
 
-        def transpose_last(c):
-            p_t = bank()
+        def transpose_last(p_t, c):
+            words = means[:].bitcast(F32).rearrange("p (c u w) -> p c u w", c=PASSES, u=HALVES)
             for u in range(HALVES):
-                for e in range(PAIR):
-                    nc.tensor.transpose(out=p_t[:, u, e, :], in_=total[:, c, u, e, :], identity=ident[:])
-            return p_t
+                nc.tensor.transpose(out=p_t[:, c, u, :], in_=words[:, c, u, :], identity=ident[:])
+
+        def copy_last(engine_copy, p_t):
+            words = p_grouped[:].rearrange("p c j f -> p (c j f)").bitcast(F32)
+            dst = words.rearrange("p (c j u) -> p c j u", c=PASSES, u=HALVES)[:, :, P:N, :]
+            engine_copy(out=dst, in_=p_t[:].rearrange("p c u j -> p c j u"))
 
         def transpose_end(p_t):
             for e in range(PAIR):
@@ -175,7 +204,7 @@ def tile_proto_metric_s_kernel(tc, x1, x2, out):
 
         def square_last():
             nc.scalar.activation(
-                out=p_squares[:], in_=total[:].rearrange("p c u e w -> p (c u e w)"), func=ACT.Square,
+                out=p_squares[:], in_=total[:], func=ACT.Square,
                 scale=1.0 / SHOT, accum_out=p_sq_last[:],
             )
 
@@ -200,8 +229,9 @@ def tile_proto_metric_s_kernel(tc, x1, x2, out):
                     )
 
         def reduce_squares(p_sq_t):
-            nc.vector.tensor_reduce(
-                out=p_sq_summed[:], in_=p_sq_t[:, 0, 0, :], axis=mybir.AxisListType.X, op=ALU.add
+            nc.vector.tensor_scalar(
+                out=p_sq_parts[:], in0=p_sq_t[:, 0, 0, :], scalar1=1.0, scalar2=p_sq_end[:], op0=ALU.mult, op1=ALU.add,
+                accum_out=p_sq_summed[:],
             )
 
         def spread(dst, parts):
@@ -214,9 +244,12 @@ def tile_proto_metric_s_kernel(tc, x1, x2, out):
         def load_query_pair():
             nc.sync.dma_start(out=x1_sb[:, 2 * D :], in_=x1_rows[:, 2 * D :])
 
-        def cross_term(i, j0=0, j1=N):
+        def cross_bank():
             tile = bank()
-            cross = tile[:].rearrange("p u e j -> p (u e j)")[:, 0 : j1 - j0]
+            return tile[:].rearrange("p u e j -> p (u e j)")
+
+        def cross_term(tile, i, j0=0, j1=N):
+            cross = tile[:, j0:j1]
             for c in range(PASSES):
                 nc.tensor.matmul_mx(
                     out=cross,
@@ -227,11 +260,10 @@ def tile_proto_metric_s_kernel(tc, x1, x2, out):
                     start=(c == 0),
                     stop=(c == PASSES - 1),
                 )
-            return cross
 
         def finish(i, cross, j0=0, j1=N):
             nc.vector.scalar_tensor_tensor(
-                out=score[:, i, j0:j1], in0=cross, scalar=q_sq[:, i : i + 1], in1=p_sq_rows[:, j0:j1],
+                out=score[:, i, j0:j1], in0=cross[:, j0:j1], scalar=q_sq[:, i : i + 1], in1=p_sq_rows[:, j0:j1],
                 op0=ALU.subtract, op1=ALU.subtract,
             )
             nc.sync.dma_start(out=out_rows[:, i, j0:j1], in_=score[:, i, j0:j1])
@@ -250,87 +282,98 @@ def tile_proto_metric_s_kernel(tc, x1, x2, out):
         with tc.manual_schedule():
             make_identity(nc, ident[:])
             make_chooser()
+            quantise_idle()
             nc.vector.memset(rows_few[:], 0.0)
+            load_queries(0)
             load_first_shots(0)
             load_first_shots(1)
             load_shot(2)
             load_shot(3)
-            load_queries(0)
-            load_shot(4)
-            load_rows(5)
-            load_rows(0)
             load_end()
+            load_rows(5)
+            load_queries(1)
+            load_shot(4)
+            load_rows(0)
             load_rows(1)
             load_rows(2)
             load_rows(3)
             load_rows(4)
-            load_queries(1)
             load_queries(2)
             load_queries(3)
             q_t0 = transpose_queries(0)
+            warm_up(16)
             first = [bank(), bank()]
             sum_rows(5, first)
-            sum_rows(0, first)
-            copy_queries(nc.scalar.copy, 0, q_t0)
+            q_t1 = transpose_queries(1)
             square_queries(0)
+            copy_queries(nc.scalar.copy, 0, q_t0)
+            square_queries(1)
+            copy_queries(nc.scalar.copy, 1, q_t1)
             add_shot(1, 0)
             add_shot(1, 1)
             add_shot(2, 0)
             add_shot(2, 1)
             add_shot(3, 0)
+            add_end(1)
             add_shot(3, 1)
+            add_end(2)
             add_shot(4, 0)
             add_shot(4, 1)
-            add_end(1)
-            quantise_queries(0)
-            add_end(2)
-            last_0 = transpose_last(0)
-            last_1 = transpose_last(1)
+            add_end(3)
+            round_means(0)
+            add_end(4)
+            round_means(1)
+            square_last()
+            sum_rows(0, first)
             sum_rows(1, first)
+            warm_up(4)
             sum_rows(2, first)
             sum_rows(3, first)
             sum_rows(4, first)
-            square_last()
-            copy_protos("scalar", 1, 1, last_1)
-            copy_protos("vector", 1, 0, last_0)
-            add_end(3)
-            quantise_protos(1, 0)
-            add_end(4)
-            copy_protos("vector", 0, 0, first[0])
-            quantise_protos(0, 0)
+            last = bank()
+            transpose_last(last, 0)
+            transpose_last(last, 1)
             transpose_end(first[1])
             rows = bank()
-            spread(rows[:, 0, 1, :], [p_sq_last])
-            q_t1 = transpose_queries(1)
             q_t2 = transpose_queries(2)
-            square_end()
-            square_summed(1, first[1])
-            square_summed(0, first[0])
-            copy_queries(nc.scalar.copy, 1, q_t1)
-            square_queries(1)
-            square_queries(2)
-            square_queries(3)
-            copy_protos("vector", 0, 1, first[1])
-            quantise_protos(1, 1)
-            copy_queries(nc.vector.tensor_copy, 2, q_t2)
-            quantise_protos(0, 1)
+            quantise_queries(0)
             quantise_queries(1)
+            square_summed(0, first[0])
+            copy_last(nc.vector.tensor_copy, last)
+            square_summed(1, first[1])
+            copy_protos("vector", 0, 0, first[0])
+            square_end()
+            copy_protos("scalar", 0, 1, first[1])
+            copy_queries(nc.scalar.copy, 2, q_t2)
+            quantise_protos(1, 0)
+            quantise_protos(1, 1)
+            quantise_protos(0, 0)
+            spread(rows[:, 0, 1, :], [p_sq_last])
+            warm_up(4)
             p_sq_t = bank()
             transpose_squares(p_sq_t)
             q_t3 = transpose_queries(3)
+            quantise_protos(0, 1)
             reduce_squares(p_sq_t)
             quantise_queries(2)
             copy_queries(nc.vector.tensor_copy, 3, q_t3)
-            spread(rows[:, 0, 0, :], [p_sq_end, p_sq_summed])
-            cross_0 = cross_term(0)
-            cross_1 = cross_term(1)
-            cross_2 = cross_term(2)
+            square_queries(2)
+            square_queries(3)
+            cross_0 = cross_bank()
+            cross_term(cross_0, 0)
+            spread(rows[:, 0, 0, :], [p_sq_summed])
+            cross_1 = cross_bank()
+            cross_term(cross_1, 1)
+            cross_2 = cross_bank()
+            cross_term(cross_2, 2)
             nc.vector.tensor_copy(out=p_sq_rows[:], in_=rows[:, 0].rearrange("p t j -> p (t j)"))
             quantise_queries(3)
             finish(0, cross_0)
             finish(1, cross_1)
             finish(2, cross_2)
-            cross_3a = cross_term(3, P, N)
-            cross_3b = cross_term(3, 0, P)
+            cross_3a = cross_bank()
+            cross_term(cross_3a, 3, P, N)
+            cross_3b = cross_bank()
+            cross_term(cross_3b, 3, 0, P)
             finish(3, cross_3a, P, N)
             finish(3, cross_3b, 0, P)

@@ -284,15 +284,15 @@ def tile_proto_metric_s_kernel(tc, x1, x2, out):
             make_chooser()
             quantise_idle()
             nc.vector.memset(rows_few[:], 0.0)
-            load_queries(0)
             load_first_shots(0)
             load_first_shots(1)
             load_shot(2)
+            load_queries(0)
             load_shot(3)
-            load_end()
-            load_rows(5)
             load_queries(1)
             load_shot(4)
+            load_end()
+            load_rows(5)
             load_rows(0)
             load_rows(1)
             load_rows(2)
@@ -300,11 +300,13 @@ def tile_proto_metric_s_kernel(tc, x1, x2, out):
             load_rows(4)
             load_queries(2)
             load_queries(3)
+            warm_up(8)
             q_t0 = transpose_queries(0)
-            warm_up(16)
+            warm_up(6)
+            q_t1 = transpose_queries(1)
+            warm_up(6)
             first = [bank(), bank()]
             sum_rows(5, first)
-            q_t1 = transpose_queries(1)
             square_queries(0)
             copy_queries(nc.scalar.copy, 0, q_t0)
             square_queries(1)
@@ -314,15 +316,17 @@ def tile_proto_metric_s_kernel(tc, x1, x2, out):
             add_shot(2, 0)
             add_shot(2, 1)
             add_shot(3, 0)
-            add_end(1)
             add_shot(3, 1)
-            add_end(2)
             add_shot(4, 0)
             add_shot(4, 1)
-            add_end(3)
+            add_end(1)
             round_means(0)
-            add_end(4)
+            add_end(2)
             round_means(1)
+            add_end(3)
+            quantise_queries(0)
+            add_end(4)
+            quantise_queries(1)
             square_last()
             sum_rows(0, first)
             sum_rows(1, first)
@@ -336,8 +340,6 @@ def tile_proto_metric_s_kernel(tc, x1, x2, out):
             transpose_end(first[1])
             rows = bank()
             q_t2 = transpose_queries(2)
-            quantise_queries(0)
-            quantise_queries(1)
             square_summed(0, first[0])
             copy_last(nc.vector.tensor_copy, last)
             square_summed(1, first[1])

@@ -300,11 +300,11 @@ def tile_proto_metric_s_kernel(tc, x1, x2, out):
             load_rows(4)
             load_queries(2)
             load_queries(3)
-            warm_up(8)
+            warm_up(11)
             q_t0 = transpose_queries(0)
-            warm_up(6)
+            warm_up(4)
             q_t1 = transpose_queries(1)
-            warm_up(6)
+            warm_up(4)
             first = [bank(), bank()]
             sum_rows(5, first)
             square_queries(0)
@@ -360,7 +360,6 @@ def tile_proto_metric_s_kernel(tc, x1, x2, out):
             quantise_queries(2)
             copy_queries(nc.vector.tensor_copy, 3, q_t3)
             square_queries(2)
-            square_queries(3)
             cross_0 = cross_bank()
             cross_term(cross_0, 0)
             spread(rows[:, 0, 0, :], [p_sq_summed])
@@ -368,7 +367,8 @@ def tile_proto_metric_s_kernel(tc, x1, x2, out):
             cross_term(cross_1, 1)
             cross_2 = cross_bank()
             cross_term(cross_2, 2)
-            nc.vector.tensor_copy(out=p_sq_rows[:], in_=rows[:, 0].rearrange("p t j -> p (t j)"))
+            nc.scalar.copy(out=p_sq_rows[:], in_=rows[:, 0].rearrange("p t j -> p (t j)"))
+            square_queries(3)
             quantise_queries(3)
             finish(0, cross_0)
             finish(1, cross_1)

@@ -289,8 +289,8 @@ def tile_proto_metric_s_kernel(tc, x1, x2, out):
             load_shot(2)
             load_queries(0)
             load_shot(3)
-            load_queries(1)
             load_shot(4)
+            load_queries(1)
             load_end()
             load_rows(5)
             load_rows(0)
@@ -329,29 +329,29 @@ def tile_proto_metric_s_kernel(tc, x1, x2, out):
             quantise_queries(1)
             square_last()
             sum_rows(0, first)
+            warm_up(3)
             sum_rows(1, first)
-            warm_up(4)
             sum_rows(2, first)
-            sum_rows(3, first)
-            sum_rows(4, first)
             last = bank()
             transpose_last(last, 0)
+            sum_rows(3, first)
             transpose_last(last, 1)
+            sum_rows(4, first)
             transpose_end(first[1])
             rows = bank()
+            spread(rows[:, 0, 1, :], [p_sq_last])
+            warm_up(4)
             q_t2 = transpose_queries(2)
+            square_end()
             square_summed(0, first[0])
             copy_last(nc.vector.tensor_copy, last)
             square_summed(1, first[1])
             copy_protos("vector", 0, 0, first[0])
-            square_end()
             copy_protos("scalar", 0, 1, first[1])
             copy_queries(nc.scalar.copy, 2, q_t2)
             quantise_protos(1, 0)
             quantise_protos(1, 1)
             quantise_protos(0, 0)
-            spread(rows[:, 0, 1, :], [p_sq_last])
-            warm_up(4)
             p_sq_t = bank()
             transpose_squares(p_sq_t)
             q_t3 = transpose_queries(3)

@@ -336,12 +336,12 @@ def tile_proto_metric_s_kernel(tc, x1, x2, out):
             transpose_last(last, 0)
             sum_rows(3, first)
             transpose_last(last, 1)
-            sum_rows(4, first)
             transpose_end(first[1])
-            rows = bank()
-            spread(rows[:, 0, 1, :], [p_sq_last])
+            sum_rows(4, first)
             warm_up(4)
             q_t2 = transpose_queries(2)
+            rows = bank()
+            spread(rows[:, 0, 1, :], [p_sq_last])
             square_end()
             square_summed(0, first[0])
             copy_last(nc.vector.tensor_copy, last)

import concourse.mybir as mybir
from concourse.masks import make_identity

F32 = mybir.dt.float32
BF16 = mybir.dt.bfloat16
U32 = mybir.dt.uint32
U8 = mybir.dt.uint8
FP8X4 = mybir.dt.float8_e4m3fn_x4
ALU = mybir.AluOpType
ACT = mybir.ActivationFunctionType

P = 128
PACK = 4
K_PASS = P * PACK

B, N, SHOT, D = 512, 256, 5, 1024
Q_TILES = B // P
PASSES = D // K_PASS
HALVES = 2
PAIR = 2
RUN = PAIR * P

SUMMED = 3 * RUN
GROUPS = [25, 25, 25, 25, 25, 3]
FEW_ROWS = 16
GROUP_STARTS = [sum(GROUPS[:g]) for g in range(len(GROUPS))]
GROUP_MAX = max(GROUPS)

FLOPS = 2 * B * N * D


def tile_proto_metric_s_kernel(tc, x1, x2, out):
    nc = tc.nc

    x1_rows = x1.rearrange("(p t) d a b -> p (t d a b)", t=Q_TILES)
    x2_shots = x2.rearrange("(t p) s d a b -> t p s (d a b)", p=P)
    x2_rows = x2.rearrange("n s d a b -> (n s) (d a b)")
    out_rows = out.rearrange("(p t) j -> p t j", t=Q_TILES)

    with tc.tile_pool(name="keep", bufs=1) as keep, tc.psum_pool(name="psum", bufs=1) as psum:
        x1_sb = keep.tile([P, Q_TILES * D], BF16)
        shots_01 = [keep.tile([P, 2, K_PASS], BF16, name=f"shots_01_{c}") for c in range(PASSES)]
        shots_24 = keep.tile([P, SHOT - 2, D], BF16)
        shots_end = keep.tile([P, SHOT, RUN], BF16)
        rows_sb = [keep.tile([P, SUMMED], BF16, name=f"rows_{g}") for g in range(len(GROUPS))]
        rows_few = rows_sb[-1]
        ident = keep.tile([P, P], F32)
        chooser = keep.tile([P, GROUP_MAX], BF16)
        total = keep.tile([P, D], F32)
        total_end = keep.tile([P, PAIR, P], F32)
        q_squares = keep.tile([P, Q_TILES * D], BF16)
        p_squares = keep.tile([P, D], BF16)
        p_squares_end = keep.tile([P, RUN], BF16)
        squares = keep.tile([P, 3, PAIR, P], F32)
        q_sq = keep.tile([P, Q_TILES], F32)
        p_sq_last = keep.tile([P, 1], F32)
        p_sq_end = keep.tile([P, 1], F32)
        p_sq_summed = keep.tile([P, 1], F32)
        p_sq_parts = keep.tile([P, P], F32)
        p_sq_rows = keep.tile([P, N], F32)
        score = keep.tile([P, Q_TILES, N], F32)
        q_grouped = keep.tile([P, Q_TILES * PASSES * P * PACK], BF16, align_bytes=64)
        q_codes = keep.tile([P, Q_TILES, PASSES, P], U32, align_bytes=64)
        q_scales = keep.tile([P, Q_TILES, PASSES, P], U8, align_bytes=64)
        p_grouped = keep.tile([P, PASSES, N, PACK], BF16, align_bytes=64)
        means = keep.tile([P, D], BF16)
        p_codes = keep.tile([P, PASSES, N], U32, align_bytes=64)
        p_scales = keep.tile([P, PASSES, N], U8, align_bytes=64)

        x1_words = x1_sb[:].bitcast(F32).rearrange(
            "p (t c u w) -> p t c u w", t=Q_TILES, c=PASSES, u=HALVES
        )
        q_grouped_words = q_grouped[:].bitcast(F32).rearrange(
            "p (t c i u) -> p t c i u", t=Q_TILES, c=PASSES, u=HALVES
        )
        q_grouped_tiles = q_grouped[:].rearrange("p (t k) -> p t k", t=Q_TILES)
        x1_tiles = x1_sb[:].rearrange("p (t d) -> p t d", t=Q_TILES)
        q_squares_tiles = q_squares[:].rearrange("p (t d) -> p t d", t=Q_TILES)

        def bank():
            return psum.tile([P, HALVES, PAIR, P], F32, name="bank", bufs=7)

        idle_in = keep.tile([P, PACK * N], BF16, align_bytes=64)
        idle_codes = keep.tile([P, N], U32, align_bytes=64)
        idle_scales = keep.tile([P, N], U8, align_bytes=64)
        idle_bank = psum.tile([P, N], F32, name="idle_bank", bufs=1)

        def quantise_idle():
            nc.vector.memset(idle_in[:], 0.0)
            nc.vector.quantize_mx(
                out=idle_codes[:].bitcast(FP8X4), scales=idle_scales[:], in_=idle_in[:]
            )

        def warm_up(times):
            for k in range(times):
                nc.tensor.matmul_mx(
                    out=idle_bank[:], lhsT=idle_codes[:, 0:P].bitcast(FP8X4), lhsT_scale=idle_scales[:, 0:P],
                    rhs=idle_codes[:].bitcast(FP8X4), rhs_scale=idle_scales[:], start=True, stop=True,
                )

        def pass_cols(c):
            return slice(c * K_PASS, (c + 1) * K_PASS)

        def load_queries(t):
            nc.sync.dma_start(out=x1_sb[:, t * D : (t + 1) * D], in_=x1_rows[:, t * D : (t + 1) * D])

        def load_first_shots(c):
            nc.sync.dma_start(out=shots_01[c][:], in_=x2_shots[1][:, 0:2, pass_cols(c)])

        def load_shot(s):
            nc.sync.dma_start(out=shots_24[:, s - 2, :], in_=x2_shots[1][:, s, :])

        def load_end():
            nc.sync.dma_start(out=shots_end[:], in_=x2_shots[0][:, :, SUMMED:D])

        def load_rows(g):
            r = SHOT * GROUP_STARTS[g]
            rows = FEW_ROWS if g == len(GROUPS) - 1 else P
            nc.sync.dma_start(out=rows_sb[g][0:rows, :], in_=x2_rows[r : r + rows, 0:SUMMED])

        def shot_part(s, c):
            return shots_01[c][:, s, :] if s < 2 else shots_24[:, s - 2, pass_cols(c)]

        def add_shot(s, c):
            part = total[:, pass_cols(c)]
            so_far = shot_part(0, c) if s == 1 else part
            nc.vector.tensor_tensor(out=part, in0=so_far, in1=shot_part(s, c), op=ALU.add)

        def add_whole_shot(s):
            nc.vector.tensor_tensor(out=total[:], in0=total[:], in1=shots_24[:, s - 2, :], op=ALU.add)

        def round_means(c):
            nc.vector.tensor_scalar_mul(out=means[:, pass_cols(c)], in0=total[:, pass_cols(c)], scalar1=2.0 / SHOT)

        def sorted_end(s):
            return shots_end[:, s, :].rearrange("p (w e) -> p e w", e=PAIR)

        def add_end(s):
            so_far = sorted_end(0) if s == 1 else total_end[:]
            nc.vector.tensor_tensor(out=total_end[:], in0=so_far, in1=sorted_end(s), op=ALU.add)

        def transpose_last(p_t, c):
            words = means[:].bitcast(F32).rearrange("p (c u w) -> p c u w", c=PASSES, u=HALVES)
            for u in range(HALVES):
                nc.tensor.transpose(out=p_t[:, c, u, :], in_=words[:, c, u, :], identity=ident[:])

        def copy_last(engine_copy, p_t):
            words = p_grouped[:].rearrange("p c j f -> p (c j f)").bitcast(F32)
            dst = words.rearrange("p (c j u) -> p c j u", c=PASSES, u=HALVES)[:, :, P:N, :]
            engine_copy(out=dst, in_=p_t[:].rearrange("p c u j -> p c j u"))

        def transpose_end(p_t):
            for e in range(PAIR):
                nc.tensor.transpose(out=p_t[:, 1, e, :], in_=total_end[:, e, :], identity=ident[:])

        def sum_rows(g, banks):
            n0, n = GROUP_STARTS[g], GROUPS[g]
            run_cols = rows_sb[g][:].rearrange("p (r w e) -> p r e w", r=3, e=PAIR)
            for r in range(3):
                for e in range(PAIR):
                    nc.tensor.matmul(
                        out=banks[r // 2][:, r % 2, e, n0 : n0 + n], lhsT=run_cols[:, r, e, :],
                        rhs=chooser[:, 0:n], start=True, stop=True,
                    )

        def copy_protos(engine, half, c, p_t):
            dst = p_grouped[:, c, half * P : (half + 1) * P, :]
            src = p_t[:].rearrange("p u e j -> p j (u e)")
            if engine == "vector":
                nc.vector.tensor_scalar_mul(out=dst, in0=src, scalar1=2.0 / SHOT)
            else:
                nc.scalar.activation(out=dst, in_=src, func=ACT.Copy, scale=2.0 / SHOT)

        def quantise_protos(half, c):
            cols = slice(half * P, (half + 1) * P)
            nc.vector.quantize_mx(
                out=p_codes[:, c, cols].bitcast(FP8X4),
                scales=p_scales[:, c, cols],
                in_=p_grouped[:, c, cols, :].rearrange("p j f -> p (j f)"),
            )

        def square_queries(t):
            nc.scalar.activation(
                out=q_squares_tiles[:, t, :], in_=x1_tiles[:, t, :], func=ACT.Square,
                accum_out=q_sq[:, t : t + 1],
            )

        def transpose_queries(t):
            q_t = bank()
            for c in range(PASSES):
                for u in range(HALVES):
                    nc.tensor.transpose(out=q_t[:, c, u, :], in_=x1_words[:, t, c, u, :], identity=ident[:])
            return q_t

        def copy_queries(engine_copy, t, q_t):
            engine_copy(out=q_grouped_words[:, t], in_=q_t[:].rearrange("p c u i -> p c i u"))

        def quantise_queries(t):
            nc.vector.quantize_mx(
                out=q_codes[:, t].rearrange("p c i -> p (c i)").bitcast(FP8X4),
                scales=q_scales[:, t].rearrange("p c i -> p (c i)"),
                in_=q_grouped_tiles[:, t, :],
            )

        def square_last():
            nc.scalar.activation(
                out=p_squares[:], in_=total[:], func=ACT.Square,
                scale=1.0 / SHOT, accum_out=p_sq_last[:],
            )

        def square_end():
            nc.scalar.activation(
                out=p_squares_end[:], in_=total_end[:].rearrange("p e w -> p (e w)"), func=ACT.Square,
                scale=1.0 / SHOT, accum_out=p_sq_end[:],
            )

        def square_summed(c, p_t):
            runs = HALVES - c
            nc.scalar.activation(
                out=squares[:, 2 * c : 2 * c + runs], in_=p_t[:, 0:runs], func=ACT.Square, scale=1.0 / SHOT
            )

        def transpose_squares(p_sq_t):
            for r in range(3):
                for e in range(PAIR):
                    nc.tensor.matmul(
                        out=p_sq_t[:, 0, 0, :], lhsT=squares[:, r, e, :], rhs=ident[:],
                        start=(r + e == 0), stop=(r + e == 3), is_transpose=True,
                    )

        def reduce_squares(p_sq_t):
            nc.vector.tensor_scalar(
                out=p_sq_parts[:], in0=p_sq_t[:, 0, 0, :], scalar1=1.0, scalar2=p_sq_end[:], op0=ALU.mult, op1=ALU.add,
                accum_out=p_sq_summed[:],
            )

        def spread(dst, parts):
            for k, part in enumerate(parts):
                nc.tensor.matmul(
                    out=dst, lhsT=part[:].to_broadcast([P, P]), rhs=ident[:],
                    start=(k == 0), stop=(k == len(parts) - 1), is_transpose=True,
                )

        def load_query_pair():
            nc.sync.dma_start(out=x1_sb[:, 2 * D :], in_=x1_rows[:, 2 * D :])

        def cross_bank():
            tile = bank()
            return tile[:].rearrange("p u e j -> p (u e j)")

        def cross_term(tile, i, j0=0, j1=N):
            cross = tile[:, j0:j1]
            for c in range(PASSES):
                nc.tensor.matmul_mx(
                    out=cross,
                    lhsT=q_codes[:, i, c, :].bitcast(FP8X4),
                    lhsT_scale=q_scales[:, i, c, :],
                    rhs=p_codes[:, c, j0:j1].bitcast(FP8X4),
                    rhs_scale=p_scales[:, c, j0:j1],
                    start=(c == 0),
                    stop=(c == PASSES - 1),
                )

        def finish(i, cross, j0=0, j1=N):
            nc.vector.scalar_tensor_tensor(
                out=score[:, i, j0:j1], in0=cross[:, j0:j1], scalar=q_sq[:, i : i + 1], in1=p_sq_rows[:, j0:j1],
                op0=ALU.subtract, op1=ALU.subtract,
            )
            nc.sync.dma_start(out=out_rows[:, i, j0:j1], in_=score[:, i, j0:j1])

        def make_chooser():
            nc.gpsimd.memset(chooser[:], 1.0)
            nc.gpsimd.affine_select(
                out=chooser[:], in_=chooser[:], pattern=[[-SHOT, GROUP_MAX]], compare_op=ALU.is_ge,
                fill=0.0, base=0, channel_multiplier=1,
            )
            nc.gpsimd.affine_select(
                out=chooser[:], in_=chooser[:], pattern=[[SHOT, GROUP_MAX]], compare_op=ALU.is_ge,
                fill=0.0, base=SHOT - 1, channel_multiplier=-1,
            )

        with tc.manual_schedule():
            make_identity(nc, ident[:])
            make_chooser()
            quantise_idle()
            nc.vector.memset(rows_few[:], 0.0)
            load_first_shots(0)
            load_first_shots(1)
            load_shot(2)
            load_queries(0)
            load_shot(3)
            load_shot(4)
            load_queries(1)
            load_end()
            load_rows(5)
            load_rows(0)
            load_rows(1)
            load_rows(2)
            load_rows(3)
            load_rows(4)
            load_queries(2)
            load_queries(3)
            warm_up(11)
            q_t0 = transpose_queries(0)
            warm_up(4)
            q_t1 = transpose_queries(1)
            warm_up(4)
            first = [bank(), bank()]
            sum_rows(5, first)
            square_queries(0)
            copy_queries(nc.scalar.copy, 0, q_t0)
            square_queries(1)
            copy_queries(nc.scalar.copy, 1, q_t1)
            add_shot(1, 0)
            add_shot(1, 1)
            add_shot(2, 0)
            add_shot(2, 1)
            add_shot(3, 0)
            add_shot(3, 1)
            add_shot(4, 0)
            add_shot(4, 1)
            add_end(1)
            round_means(0)
            add_end(2)
            round_means(1)
            add_end(3)
            quantise_queries(0)
            add_end(4)
            quantise_queries(1)
            square_last()
            sum_rows(0, first)
            warm_up(3)
            sum_rows(1, first)
            sum_rows(2, first)
            last = bank()
            transpose_last(last, 0)
            sum_rows(3, first)
            transpose_last(last, 1)
            transpose_end(first[1])
            sum_rows(4, first)
            warm_up(4)
            q_t2 = transpose_queries(2)
            rows = bank()
            spread(rows[:, 0, 1, :], [p_sq_last])
            square_end()
            square_summed(0, first[0])
            copy_last(nc.vector.tensor_copy, last)
            square_summed(1, first[1])
            copy_protos("vector", 0, 0, first[0])
            copy_protos("scalar", 0, 1, first[1])
            copy_queries(nc.scalar.copy, 2, q_t2)
            quantise_protos(1, 0)
            quantise_protos(1, 1)
            quantise_protos(0, 0)
            p_sq_t = bank()
            transpose_squares(p_sq_t)
            q_t3 = transpose_queries(3)
            quantise_protos(0, 1)
            reduce_squares(p_sq_t)
            quantise_queries(2)
            copy_queries(nc.vector.tensor_copy, 3, q_t3)
            square_queries(2)
            cross_0 = cross_bank()
            cross_term(cross_0, 0)
            spread(rows[:, 0, 0, :], [p_sq_summed])
            cross_1 = cross_bank()
            cross_term(cross_1, 1)
            cross_2 = cross_bank()
            cross_term(cross_2, 2)
            nc.scalar.copy(out=p_sq_rows[:], in_=rows[:, 0].rearrange("p t j -> p (t j)"))
            square_queries(3)
            quantise_queries(3)
            finish(0, cross_0)
            finish(1, cross_1)
            finish(2, cross_2)
            cross_3a = cross_bank()
            cross_term(cross_3a, 3, P, N)
            cross_3b = cross_bank()
            cross_term(cross_3b, 3, 0, P)
            finish(3, cross_3a, P, N)
            finish(3, cross_3b, 0, P)
